import numpy as np
import ml_dtypes


BF16 = ml_dtypes.bfloat16


def bf(x):
    return np.asarray(x, np.float32).astype(BF16)


def f64(x):
    return np.asarray(x).astype(np.float64)


E2M1 = np.array([0.0, 0.5, 1.0, 1.5, 2.0, 3.0, 4.0, 6.0, -0.0, -0.5, -1.0, -1.5, -2.0, -3.0, -4.0, -6.0])


def pack_weight(w, fmt):
    k, n = w.shape
    w = f64(bf(w)).reshape(k // 32, 32, n)
    amax = np.abs(w).max(1)
    if fmt == "e4m3":
        byte = np.frexp(amax)[1] - 1 + 127 - 7
    else:
        mant, ex = np.frexp(amax / 6.0)
        byte = np.where(mant > 0.5, ex, ex - 1) + 127
    byte = np.clip(np.where(amax > 0, byte, 1), 1, 254)
    scaled = (w * np.exp2(127.0 - byte)[:, None, :]).reshape(k, n).astype(np.float32)
    by_word = np.ascontiguousarray(scaled.reshape(k // 512, 128, 4, n).transpose(0, 1, 3, 2))
    if fmt == "e4m3":
        words = by_word.astype(ml_dtypes.float8_e4m3fn).view(np.uint8)
    else:
        c = by_word.astype(ml_dtypes.float4_e2m1fn).view(np.uint8) & 0xF
        words = c[..., 0::2] | (c[..., 1::2] << 4)
    return np.ascontiguousarray(words), np.ascontiguousarray(byte.astype(np.uint8).reshape(k // 512, 16, n))


def unpack_weight(words, scales, fmt):
    g, p, n, _ = words.shape
    if fmt == "e4m3":
        vals = np.ascontiguousarray(words).view(ml_dtypes.float8_e4m3fn).astype(np.float64)
    else:
        nib = np.empty((g, p, n, 4), np.uint8)
        nib[..., 0::2] = words & 0xF
        nib[..., 1::2] = words >> 4
        vals = E2M1[nib]
    vals = vals * np.repeat(np.exp2(scales.astype(np.float64) - 127.0), 8, axis=1)[..., None]
    return vals.transpose(0, 1, 3, 2).reshape(g * 512, n)

def pack4(w):
    words, scales = pack_weight(w, "e2m1")
    return words.reshape(words.shape[0], 128, -1), scales


def unpack4(words, scales):
    return unpack_weight(words.reshape(words.shape[0], 128, -1, 2), scales, "e2m1")


def kspread(k):
    return np.exp2(np.repeat(np.random.randint(-6, 7, k // 32), 32).astype(np.float64))


B, L, F, D, N = 128, 32, 4096, 1024, 8192
TOP = 0.8 * np.sqrt(2.0 * np.log(L))


def elu(v):
    return np.where(v > 0.0, v, np.exp(np.minimum(v, 0.0)) - 1.0)


def setup_inputs():
    s = kspread(F)
    x = np.random.standard_normal((B, L, F)) * s
    x_words, x_scales = pack4(x.reshape(B * L, F).T)
    words, scales = pack4((np.random.standard_normal((D, F)) / np.sqrt(F) / s).T)
    conv_b = bf(np.random.standard_normal(D) * 2.0 - TOP)
    return {"x_words": x_words,
            "x_scales": x_scales,
            "conv_w_words": words,
            "conv_w_scales": scales,
            "conv_b": conv_b}


def reference(x_words, x_scales, conv_w_words, conv_w_scales, conv_b):
    z = (unpack4(x_words, x_scales).T.reshape(B, L, F) @ unpack4(conv_w_words, conv_w_scales)) + f64(conv_b)
    return elu(z).max(axis=1)

@@ -1,0 +1,193 @@
+from contextlib import ExitStack
+
+import concourse.masks as masks
+import concourse.mybir as mybir
+
+FLOPS = 2 * 4096 * 1024 * 4096
+
+F32 = mybir.dt.float32
+BF16 = mybir.dt.bfloat16
+I32 = mybir.dt.int32
+U8 = mybir.dt.uint8
+FP4X4 = mybir.dt.float4_e2m1fn_x4
+ALU = mybir.AluOpType
+
+P = 128
+PASSES = 8
+SEQ = 32
+N_TILE = 512
+ROW_BLOCKS = 8
+CH_BLOCKS = 8
+SEQ_PER_TILE = N_TILE // SEQ
+
+GROUPS = ((0, 1, 2, 3), (4, 5, 6), (7,))
+
+
+def tile_conceptembedmodel_pa_kernel(tc, x_words, x_scales, conv_w_words, conv_w_scales, conv_b, out):
+    nc = tc.nc
+
+    with ExitStack() as ctx:
+        keep = ctx.enter_context(tc.tile_pool(name="keep", bufs=1))
+        psum = ctx.enter_context(tc.psum_pool(name="psum", bufs=8))
+        ctx.enter_context(tc.manual_schedule())
+
+        w_code, w_plane, x_code, x_plane = {}, {}, {}, {}
+
+        def load_codes(table, key, words, g0, g1, c0, c1, name):
+            t = keep.tile([P, g1 - g0, 2 * (c1 - c0)], U8, name=name, align_bytes=64)
+            nc.sync.dma_start(
+                out=t[:].bitcast(I32),
+                in_=words[g0:g1, :, 2 * c0 : 2 * c1].rearrange("g p n -> p g n").bitcast(I32),
+            )
+            for g in range(g0, g1):
+                table[(key, g)] = (t, g - g0)
+
+        def load_planes(table, key, scales, g0, g1, c0, c1, name):
+            t = keep.tile([P, g1 - g0, c1 - c0], U8, name=name, align_bytes=64)
+            nc.vector.memset(t[:].bitcast(I32), 0)
+            for q in range(4):
+                nc.sync.dma_start(
+                    out=t[32 * q : 32 * q + 4, :, :].bitcast(I32),
+                    in_=scales[g0:g1, 4 * q : 4 * q + 4, c0:c1].rearrange("g r n -> r g n").bitcast(I32),
+                )
+            for g in range(g0, g1):
+                table[(key, g)] = (t, g - g0)
+
+        def load_w_codes(g0, g1):
+            load_codes(w_code, 0, conv_w_words, g0, g1, 0, CH_BLOCKS * P, "wc%d" % g0)
+
+        def load_w_planes(g0, g1):
+            load_planes(w_plane, 0, conv_w_scales, g0, g1, 0, CH_BLOCKS * P, "wp%d" % g0)
+
+        def load_x_codes(r, g0, g1):
+            load_codes(x_code, r, x_words, g0, g1, N_TILE * r, N_TILE * (r + 1), "xc%d_%d" % (r, g0))
+
+        def load_x_planes(r, g0, g1):
+            load_planes(x_plane, r, x_scales, g0, g1, N_TILE * r, N_TILE * (r + 1), "xp%d_%d" % (r, g0))
+
+        ident = keep.tile([P, P], F32, name="ident")
+        masks.make_identity(nc, ident[:])
+        warm = keep.tile([P, 1], F32, name="warm")
+        nc.scalar.activation(out=warm[:], in_=ident[:, 0:1], func=mybir.ActivationFunctionType.Exp)
+
+        load_w_planes(0, 1)
+        load_x_planes(0, 0, PASSES)
+        load_w_codes(0, 1)
+        load_x_codes(0, 0, 1)
+        load_w_planes(1, 4)
+        load_w_codes(1, 2)
+        load_x_codes(0, 1, 4)
+        load_w_codes(2, 4)
+        load_w_planes(4, 8)
+        load_w_codes(4, 8)
+        load_x_codes(0, 4, 8)
+        for r in range(1, ROW_BLOCKS):
+            load_x_planes(r, 0, PASSES)
+            load_x_codes(r, 0, PASSES)
+        bias_bf = keep.tile([P, CH_BLOCKS], BF16, name="bias_bf")
+        with nc.allow_non_contiguous_dma(reason="1024 bias values, one channel to a partition"):
+            nc.sync.dma_start(out=bias_bf[:], in_=conv_b.rearrange("(c p) -> p c", p=P))
+        bias = keep.tile([P, CH_BLOCKS], F32, name="bias")
+
+        where = {}
+        peak, neg, pos, ex, val = [], [], [], [], []
+        for gi, js in enumerate(GROUPS):
+            for i, j in enumerate(js):
+                where[j] = (gi, i)
+            shape = [P, len(js), P]
+            peak.append(keep.tile(shape, F32, name="peak%d" % gi))
+            neg.append(keep.tile(shape, F32, name="neg%d" % gi))
+            pos.append(keep.tile(shape, F32, name="pos%d" % gi))
+            ex.append(keep.tile(shape, F32, name="ex%d" % gi))
+            val.append(keep.tile(shape, F32, name="val%d" % gi))
+
+        def multiply(acc, j, r, g):
+            wc, wi = w_code[(0, g)]
+            wp, wpi = w_plane[(0, g)]
+            xc, xi = x_code[(r, g)]
+            xp, xpi = x_plane[(r, g)]
+            nc.tensor.matmul_mx(
+                out=acc[:],
+                lhsT=wc[:, wi, 2 * P * j : 2 * P * (j + 1)].bitcast(FP4X4),
+                lhsT_scale=wp[:, wpi, P * j : P * (j + 1)],
+                rhs=xc[:, xi, :].bitcast(FP4X4),
+                rhs_scale=xp[:, xpi, :],
+                start=(g == 0),
+                stop=(g == PASSES - 1),
+            )
+
+        def pool_positions(acc, j, r):
+            gi, i = where[j]
+            nc.vector.tensor_reduce(
+                out=peak[gi][:, i, SEQ_PER_TILE * r : SEQ_PER_TILE * (r + 1)],
+                in_=acc[:].rearrange("p (b l) -> p b l", l=SEQ),
+                axis=mybir.AxisListType.X,
+                op=ALU.max,
+            )
+
+        def elu_halves(j):
+            gi, i = where[j]
+            nc.vector.tensor_scalar(
+                out=neg[gi][:, i, :], in0=peak[gi][:, i, :], scalar1=bias[:, j : j + 1], scalar2=0.0,
+                op0=ALU.add, op1=ALU.min,
+            )
+            nc.vector.tensor_scalar(
+                out=pos[gi][:, i, :], in0=peak[gi][:, i, :], scalar1=bias[:, j : j + 1], scalar2=0.0,
+                op0=ALU.add, op1=ALU.max,
+            )
+
+        def elu_join(gi):
+            flat = "p i b -> p (i b)"
+            nc.scalar.activation(
+                out=ex[gi][:].rearrange(flat), in_=neg[gi][:].rearrange(flat), func=mybir.ActivationFunctionType.Exp
+            )
+            nc.vector.scalar_tensor_tensor(
+                out=val[gi][:].rearrange(flat), in0=ex[gi][:].rearrange(flat), scalar=-1.0,
+                in1=pos[gi][:].rearrange(flat), op0=ALU.add, op1=ALU.add,
+            )
+
+        def turn_and_store(gi):
+            js = GROUPS[gi]
+            n = len(js)
+            flipped = psum.tile([P, N_TILE], F32, tag="acc", name="flipped%d" % gi)
+            for i in range(n):
+                nc.tensor.transpose(flipped[:, P * i : P * (i + 1)], val[gi][:, i, :], ident[:])
+            res = keep.tile([P, n * P], F32, name="res%d" % gi)
+            nc.vector.tensor_copy(out=res[:], in_=flipped[:, : n * P])
+            nc.sync.dma_start(out=out[:, P * js[0] : P * (js[0] + n)], in_=res[:])
+
+        def whole_tile(j, r):
+            acc = psum.tile([P, N_TILE], F32, tag="acc", name="acc")
+            for g in range(PASSES):
+                multiply(acc, j, r, g)
+            pool_positions(acc, j, r)
+            if r == ROW_BLOCKS - 1:
+                elu_halves(j)
+                gi, i = where[j]
+                if i == len(GROUPS[gi]) - 1:
+                    elu_join(gi)
+
+        first = []
+        for j in range(CH_BLOCKS):
+            acc0 = psum.tile([P, N_TILE], F32, tag="acc", name="acc")
+            first.append(acc0)
+        for g in range(PASSES):
+            for j in range(CH_BLOCKS):
+                multiply(first[j], j, 0, g)
+        for j in range(CH_BLOCKS):
+            pool_positions(first[j], j, 0)
+
+        for r in range(1, ROW_BLOCKS):
+            if r == ROW_BLOCKS - 1:
+                nc.vector.tensor_copy(out=bias[:], in_=bias_bf[:])
+            for j in GROUPS[0]:
+                whole_tile(j, r)
+
+        for j in range(4, CH_BLOCKS):
+            for r in range(1, ROW_BLOCKS):
+                whole_tile(j, r)
+                if r == 2 and j == 4:
+                    turn_and_store(0)
+                if r == 2 and j == 7:
+                    turn_and_store(1)
+        turn_and_store(2)

@@ -21,6 +21,7 @@ CH_BLOCKS = 8
 SEQ_PER_TILE = N_TILE // SEQ
 
 GROUPS = ((0, 1, 2, 3), (4, 5, 6), (7,))
+WARM_UP = 8
 
 
 def tile_conceptembedmodel_pa_kernel(tc, x_words, x_scales, conv_w_words, conv_w_scales, conv_b, out):
@@ -65,15 +66,12 @@ def tile_conceptembedmodel_pa_kernel(tc, x_words, x_scales, conv_w_words, conv_w
         def load_x_planes(r, g0, g1):
             load_planes(x_plane, r, x_scales, g0, g1, N_TILE * r, N_TILE * (r + 1), "xp%d_%d" % (r, g0))
 
-        ident = keep.tile([P, P], F32, name="ident")
-        masks.make_identity(nc, ident[:])
-        warm = keep.tile([P, 1], F32, name="warm")
-        nc.scalar.activation(out=warm[:], in_=ident[:, 0:1], func=mybir.ActivationFunctionType.Exp)
-
         load_w_planes(0, 1)
-        load_x_planes(0, 0, PASSES)
+        zeros = keep.tile([P, N_TILE], BF16, name="zeros")
+        nc.vector.memset(zeros[:], 0.0)
         load_w_codes(0, 1)
         load_x_codes(0, 0, 1)
+        load_x_planes(0, 0, PASSES)
         load_w_planes(1, 4)
         load_w_codes(1, 2)
         load_x_codes(0, 1, 4)
@@ -89,6 +87,16 @@ def tile_conceptembedmodel_pa_kernel(tc, x_words, x_scales, conv_w_words, conv_w
             nc.sync.dma_start(out=bias_bf[:], in_=conv_b.rearrange("(c p) -> p c", p=P))
         bias = keep.tile([P, CH_BLOCKS], F32, name="bias")
 
+        ident = keep.tile([P, P], F32, name="ident")
+        nc.vector.memset(ident[:], 0.0)
+        masks.make_identity(nc, ident[:], nomemset=True)
+        warm = keep.tile([P, 1], F32, name="warm")
+        nc.scalar.activation(out=warm[:], in_=ident[:, 0:1], func=mybir.ActivationFunctionType.Exp)
+
+        idle = psum.tile([P, N_TILE], F32, tag="acc", name="idle")
+        for k in range(WARM_UP):
+            nc.tensor.matmul(out=idle[:], lhsT=zeros[:, 0:P], rhs=zeros[:], start=True, stop=True)
+
         where = {}
         peak, neg, pos, ex, val = [], [], [], [], []
         for gi, js in enumerate(GROUPS):
@@ -101,49 +109,51 @@ def tile_conceptembedmodel_pa_kernel(tc, x_words, x_scales, conv_w_words, conv_w
             ex.append(keep.tile(shape, F32, name="ex%d" % gi))
             val.append(keep.tile(shape, F32, name="val%d" % gi))
 
-        def multiply(acc, j, r, g):
+        def multiply(acc, j, r, g, c0=0, n=N_TILE):
             wc, wi = w_code[(0, g)]
             wp, wpi = w_plane[(0, g)]
             xc, xi = x_code[(r, g)]
             xp, xpi = x_plane[(r, g)]
             nc.tensor.matmul_mx(
-                out=acc[:],
+                out=acc[:, 0:n],
                 lhsT=wc[:, wi, 2 * P * j : 2 * P * (j + 1)].bitcast(FP4X4),
                 lhsT_scale=wp[:, wpi, P * j : P * (j + 1)],
-                rhs=xc[:, xi, :].bitcast(FP4X4),
-                rhs_scale=xp[:, xpi, :],
+                rhs=xc[:, xi, 2 * c0 : 2 * (c0 + n)].bitcast(FP4X4),
+                rhs_scale=xp[:, xpi, c0 : c0 + n],
                 start=(g == 0),
                 stop=(g == PASSES - 1),
             )
 
-        def pool_positions(acc, j, r):
+        def pool_positions(acc, j, r, c0=0, n=N_TILE):
             gi, i = where[j]
+            b0 = (N_TILE * r + c0) // SEQ
             nc.vector.tensor_reduce(
-                out=peak[gi][:, i, SEQ_PER_TILE * r : SEQ_PER_TILE * (r + 1)],
-                in_=acc[:].rearrange("p (b l) -> p b l", l=SEQ),
+                out=peak[gi][:, i, b0 : b0 + n // SEQ],
+                in_=acc[:, 0:n].rearrange("p (b l) -> p b l", l=SEQ),
                 axis=mybir.AxisListType.X,
                 op=ALU.max,
             )
 
-        def elu_halves(j):
+        def elu_halves(j, b0=0, b1=P):
             gi, i = where[j]
             nc.vector.tensor_scalar(
-                out=neg[gi][:, i, :], in0=peak[gi][:, i, :], scalar1=bias[:, j : j + 1], scalar2=0.0,
+                out=neg[gi][:, i, b0:b1], in0=peak[gi][:, i, b0:b1], scalar1=bias[:, j : j + 1], scalar2=0.0,
                 op0=ALU.add, op1=ALU.min,
             )
             nc.vector.tensor_scalar(
-                out=pos[gi][:, i, :], in0=peak[gi][:, i, :], scalar1=bias[:, j : j + 1], scalar2=0.0,
+                out=pos[gi][:, i, b0:b1], in0=peak[gi][:, i, b0:b1], scalar1=bias[:, j : j + 1], scalar2=0.0,
                 op0=ALU.add, op1=ALU.max,
             )
 
-        def elu_join(gi):
+        def elu_join(gi, lo, hi):
             flat = "p i b -> p (i b)"
             nc.scalar.activation(
-                out=ex[gi][:].rearrange(flat), in_=neg[gi][:].rearrange(flat), func=mybir.ActivationFunctionType.Exp
+                out=ex[gi][:].rearrange(flat)[:, lo:hi], in_=neg[gi][:].rearrange(flat)[:, lo:hi],
+                func=mybir.ActivationFunctionType.Exp,
             )
             nc.vector.scalar_tensor_tensor(
-                out=val[gi][:].rearrange(flat), in0=ex[gi][:].rearrange(flat), scalar=-1.0,
-                in1=pos[gi][:].rearrange(flat), op0=ALU.add, op1=ALU.add,
+                out=val[gi][:].rearrange(flat)[:, lo:hi], in0=ex[gi][:].rearrange(flat)[:, lo:hi], scalar=-1.0,
+                in1=pos[gi][:].rearrange(flat)[:, lo:hi], op0=ALU.add, op1=ALU.add,
             )
 
         def turn_and_store(gi):
@@ -156,16 +166,17 @@ def tile_conceptembedmodel_pa_kernel(tc, x_words, x_scales, conv_w_words, conv_w
             nc.vector.tensor_copy(out=res[:], in_=flipped[:, : n * P])
             nc.sync.dma_start(out=out[:, P * js[0] : P * (js[0] + n)], in_=res[:])
 
-        def whole_tile(j, r):
+        def whole_tile(j, r, c0=0, n=N_TILE):
             acc = psum.tile([P, N_TILE], F32, tag="acc", name="acc")
             for g in range(PASSES):
-                multiply(acc, j, r, g)
-            pool_positions(acc, j, r)
-            if r == ROW_BLOCKS - 1:
-                elu_halves(j)
-                gi, i = where[j]
-                if i == len(GROUPS[gi]) - 1:
-                    elu_join(gi)
+                multiply(acc, j, r, g, c0, n)
+            pool_positions(acc, j, r, c0, n)
+
+        def finish_block(j):
+            elu_halves(j)
+            gi, i = where[j]
+            if i == len(GROUPS[gi]) - 1:
+                elu_join(gi, 0, P * len(GROUPS[gi]))
 
         first = []
         for j in range(CH_BLOCKS):
@@ -182,12 +193,25 @@ def tile_conceptembedmodel_pa_kernel(tc, x_words, x_scales, conv_w_words, conv_w
                 nc.vector.tensor_copy(out=bias[:], in_=bias_bf[:])
             for j in GROUPS[0]:
                 whole_tile(j, r)
+                if r == ROW_BLOCKS - 1:
+                    finish_block(j)
 
-        for j in range(4, CH_BLOCKS):
+        for j in GROUPS[1]:
             for r in range(1, ROW_BLOCKS):
                 whole_tile(j, r)
-                if r == 2 and j == 4:
-                    turn_and_store(0)
-                if r == 2 and j == 7:
-                    turn_and_store(1)
+            finish_block(j)
+
+        last = CH_BLOCKS - 1
+        early = SEQ_PER_TILE * (ROW_BLOCKS - 1)
+        for r in range(1, ROW_BLOCKS - 1):
+            whole_tile(last, r)
+            if r == 2:
+                turn_and_store(0)
+                turn_and_store(1)
+        elu_halves(last, 0, early)
+        elu_join(2, 0, early)
+        whole_tile(last, ROW_BLOCKS - 1, 0, N_TILE // 2)
+        whole_tile(last, ROW_BLOCKS - 1, N_TILE // 2, N_TILE // 2)
+        elu_halves(last, early, P)
+        elu_join(2, early, P)
         turn_and_store(2)

@@ -1,6 +1,5 @@
 from contextlib import ExitStack
 
-import concourse.masks as masks
 import concourse.mybir as mybir
 
 FLOPS = 2 * 4096 * 1024 * 4096
@@ -11,6 +10,7 @@ I32 = mybir.dt.int32
 U8 = mybir.dt.uint8
 FP4X4 = mybir.dt.float4_e2m1fn_x4
 ALU = mybir.AluOpType
+EXP = mybir.ActivationFunctionType.Exp
 
 P = 128
 PASSES = 8
@@ -18,10 +18,10 @@ SEQ = 32
 N_TILE = 512
 ROW_BLOCKS = 8
 CH_BLOCKS = 8
-SEQ_PER_TILE = N_TILE // SEQ
-
-GROUPS = ((0, 1, 2, 3), (4, 5, 6), (7,))
-WARM_UP = 8
+SIDE_BY_SIDE = 4
+SQ = 32
+WARM_N = 256
+WARM_UP = 18
 
 
 def tile_conceptembedmodel_pa_kernel(tc, x_words, x_scales, conv_w_words, conv_w_scales, conv_b, out):
@@ -66,15 +66,23 @@ def tile_conceptembedmodel_pa_kernel(tc, x_words, x_scales, conv_w_words, conv_w
         def load_x_planes(r, g0, g1):
             load_planes(x_plane, r, x_scales, g0, g1, N_TILE * r, N_TILE * (r + 1), "xp%d_%d" % (r, g0))
 
+        zeros = keep.tile([P, WARM_N], BF16, name="zeros")
+        nc.gpsimd.memset(zeros[:], 0.0)
+        idle = psum.tile([P, N_TILE], F32, tag="acc", name="idle")
+        for k in range(WARM_UP):
+            nc.tensor.matmul(out=idle[:, 0:WARM_N], lhsT=zeros[:, 0:P], rhs=zeros[:], start=True, stop=True)
+        warm = keep.tile([P, 1], F32, name="warm")
+        nc.scalar.activation(out=warm[:], in_=zeros[:, 0:1], func=EXP)
+
         load_w_planes(0, 1)
-        zeros = keep.tile([P, N_TILE], BF16, name="zeros")
-        nc.vector.memset(zeros[:], 0.0)
         load_w_codes(0, 1)
         load_x_codes(0, 0, 1)
-        load_x_planes(0, 0, PASSES)
+        load_x_planes(0, 0, 2)
         load_w_planes(1, 4)
+        load_x_codes(0, 1, 2)
         load_w_codes(1, 2)
-        load_x_codes(0, 1, 4)
+        load_x_planes(0, 2, 8)
+        load_x_codes(0, 2, 4)
         load_w_codes(2, 4)
         load_w_planes(4, 8)
         load_w_codes(4, 8)
@@ -87,29 +95,16 @@ def tile_conceptembedmodel_pa_kernel(tc, x_words, x_scales, conv_w_words, conv_w
             nc.sync.dma_start(out=bias_bf[:], in_=conv_b.rearrange("(c p) -> p c", p=P))
         bias = keep.tile([P, CH_BLOCKS], F32, name="bias")
 
-        ident = keep.tile([P, P], F32, name="ident")
-        nc.vector.memset(ident[:], 0.0)
-        masks.make_identity(nc, ident[:], nomemset=True)
-        warm = keep.tile([P, 1], F32, name="warm")
-        nc.scalar.activation(out=warm[:], in_=ident[:, 0:1], func=mybir.ActivationFunctionType.Exp)
+        peak, neg, pos, ex, val, turned = [], [], [], [], [], []
+        for j in range(CH_BLOCKS):
+            peak.append(keep.tile([P, P], F32, name="peak%d" % j))
+            neg.append(keep.tile([P, P], F32, name="neg%d" % j))
+            pos.append(keep.tile([P, P], F32, name="pos%d" % j))
+            ex.append(keep.tile([P, P], F32, name="ex%d" % j))
+            val.append(keep.tile([P, P], F32, name="val%d" % j, align_bytes=64))
+            turned.append(keep.tile([P, P], F32, name="turned%d" % j, align_bytes=64))
 
-        idle = psum.tile([P, N_TILE], F32, tag="acc", name="idle")
-        for k in range(WARM_UP):
-            nc.tensor.matmul(out=idle[:], lhsT=zeros[:, 0:P], rhs=zeros[:], start=True, stop=True)
-
-        where = {}
-        peak, neg, pos, ex, val = [], [], [], [], []
-        for gi, js in enumerate(GROUPS):
-            for i, j in enumerate(js):
-                where[j] = (gi, i)
-            shape = [P, len(js), P]
-            peak.append(keep.tile(shape, F32, name="peak%d" % gi))
-            neg.append(keep.tile(shape, F32, name="neg%d" % gi))
-            pos.append(keep.tile(shape, F32, name="pos%d" % gi))
-            ex.append(keep.tile(shape, F32, name="ex%d" % gi))
-            val.append(keep.tile(shape, F32, name="val%d" % gi))
-
-        def multiply(acc, j, r, g, c0=0, n=N_TILE):
+        def multiply(acc, j, r, g, c0, n):
             wc, wi = w_code[(0, g)]
             wp, wpi = w_plane[(0, g)]
             xc, xi = x_code[(r, g)]
@@ -124,47 +119,14 @@ def tile_conceptembedmodel_pa_kernel(tc, x_words, x_scales, conv_w_words, conv_w
                 stop=(g == PASSES - 1),
             )
 
-        def pool_positions(acc, j, r, c0=0, n=N_TILE):
-            gi, i = where[j]
+        def pool_positions(acc, j, r, c0, n):
             b0 = (N_TILE * r + c0) // SEQ
             nc.vector.tensor_reduce(
-                out=peak[gi][:, i, b0 : b0 + n // SEQ],
+                out=peak[j][:, b0 : b0 + n // SEQ],
                 in_=acc[:, 0:n].rearrange("p (b l) -> p b l", l=SEQ),
                 axis=mybir.AxisListType.X,
                 op=ALU.max,
             )
-
-        def elu_halves(j, b0=0, b1=P):
-            gi, i = where[j]
-            nc.vector.tensor_scalar(
-                out=neg[gi][:, i, b0:b1], in0=peak[gi][:, i, b0:b1], scalar1=bias[:, j : j + 1], scalar2=0.0,
-                op0=ALU.add, op1=ALU.min,
-            )
-            nc.vector.tensor_scalar(
-                out=pos[gi][:, i, b0:b1], in0=peak[gi][:, i, b0:b1], scalar1=bias[:, j : j + 1], scalar2=0.0,
-                op0=ALU.add, op1=ALU.max,
-            )
-
-        def elu_join(gi, lo, hi):
-            flat = "p i b -> p (i b)"
-            nc.scalar.activation(
-                out=ex[gi][:].rearrange(flat)[:, lo:hi], in_=neg[gi][:].rearrange(flat)[:, lo:hi],
-                func=mybir.ActivationFunctionType.Exp,
-            )
-            nc.vector.scalar_tensor_tensor(
-                out=val[gi][:].rearrange(flat)[:, lo:hi], in0=ex[gi][:].rearrange(flat)[:, lo:hi], scalar=-1.0,
-                in1=pos[gi][:].rearrange(flat)[:, lo:hi], op0=ALU.add, op1=ALU.add,
-            )
-
-        def turn_and_store(gi):
-            js = GROUPS[gi]
-            n = len(js)
-            flipped = psum.tile([P, N_TILE], F32, tag="acc", name="flipped%d" % gi)
-            for i in range(n):
-                nc.tensor.transpose(flipped[:, P * i : P * (i + 1)], val[gi][:, i, :], ident[:])
-            res = keep.tile([P, n * P], F32, name="res%d" % gi)
-            nc.vector.tensor_copy(out=res[:], in_=flipped[:, : n * P])
-            nc.sync.dma_start(out=out[:, P * js[0] : P * (js[0] + n)], in_=res[:])
 
         def whole_tile(j, r, c0=0, n=N_TILE):
             acc = psum.tile([P, N_TILE], F32, tag="acc", name="acc")
@@ -172,11 +134,29 @@ def tile_conceptembedmodel_pa_kernel(tc, x_words, x_scales, conv_w_words, conv_w
                 multiply(acc, j, r, g, c0, n)
             pool_positions(acc, j, r, c0, n)
 
-        def finish_block(j):
-            elu_halves(j)
-            gi, i = where[j]
-            if i == len(GROUPS[gi]) - 1:
-                elu_join(gi, 0, P * len(GROUPS[gi]))
+        def elu(j, b0, b1):
+            nc.vector.tensor_scalar(
+                out=neg[j][:, b0:b1], in0=peak[j][:, b0:b1], scalar1=bias[:, j : j + 1], scalar2=0.0,
+                op0=ALU.add, op1=ALU.min,
+            )
+            nc.scalar.activation(out=ex[j][:, b0:b1], in_=neg[j][:, b0:b1], func=EXP)
+            nc.vector.tensor_scalar(
+                out=pos[j][:, b0:b1], in0=peak[j][:, b0:b1], scalar1=bias[:, j : j + 1], scalar2=0.0,
+                op0=ALU.add, op1=ALU.max,
+            )
+            nc.vector.scalar_tensor_tensor(
+                out=val[j][:, b0:b1], in0=ex[j][:, b0:b1], scalar=-1.0, in1=pos[j][:, b0:b1],
+                op0=ALU.add, op1=ALU.add,
+            )
+
+        def turn_and_store(j, queues):
+            nc.vector.transpose(out=turned[j][:], in_=val[j][:])
+            for s in range(P // SQ):
+                c0 = P * j + SQ * s
+                queues[s % len(queues)].dma_start(
+                    out=out[:, c0 : c0 + SQ].rearrange("(t i) k -> i t k", i=SQ),
+                    in_=turned[j][SQ * s : SQ * (s + 1), :].rearrange("i (t k) -> i t k", k=SQ),
+                )
 
         first = []
         for j in range(CH_BLOCKS):
@@ -184,34 +164,31 @@ def tile_conceptembedmodel_pa_kernel(tc, x_words, x_scales, conv_w_words, conv_w
             first.append(acc0)
         for g in range(PASSES):
             for j in range(CH_BLOCKS):
-                multiply(first[j], j, 0, g)
+                multiply(first[j], j, 0, g, 0, N_TILE)
         for j in range(CH_BLOCKS):
-            pool_positions(first[j], j, 0)
+            pool_positions(first[j], j, 0, 0, N_TILE)
 
         for r in range(1, ROW_BLOCKS):
             if r == ROW_BLOCKS - 1:
                 nc.vector.tensor_copy(out=bias[:], in_=bias_bf[:])
-            for j in GROUPS[0]:
+            for j in range(SIDE_BY_SIDE):
                 whole_tile(j, r)
                 if r == ROW_BLOCKS - 1:
-                    finish_block(j)
-
-        for j in GROUPS[1]:
-            for r in range(1, ROW_BLOCKS):
-                whole_tile(j, r)
-            finish_block(j)
+                    elu(j, 0, P)
+                    turn_and_store(j, [nc.sync])
 
         last = CH_BLOCKS - 1
-        early = SEQ_PER_TILE * (ROW_BLOCKS - 1)
+        for j in range(SIDE_BY_SIDE, last):
+            for r in range(1, ROW_BLOCKS):
+                whole_tile(j, r)
+            elu(j, 0, P)
+            turn_and_store(j, [nc.sync])
+
+        early = (N_TILE // SEQ) * (ROW_BLOCKS - 1)
         for r in range(1, ROW_BLOCKS - 1):
             whole_tile(last, r)
-            if r == 2:
-                turn_and_store(0)
-                turn_and_store(1)
-        elu_halves(last, 0, early)
-        elu_join(2, 0, early)
+        elu(last, 0, early)
         whole_tile(last, ROW_BLOCKS - 1, 0, N_TILE // 2)
         whole_tile(last, ROW_BLOCKS - 1, N_TILE // 2, N_TILE // 2)
-        elu_halves(last, early, P)
-        elu_join(2, early, P)
-        turn_and_store(2)
+        elu(last, early, P)
+        turn_and_store(last, [nc.sync, nc.scalar])

@@ -20,8 +20,7 @@ ROW_BLOCKS = 8
 CH_BLOCKS = 8
 SIDE_BY_SIDE = 4
 SQ = 32
-WARM_N = 256
-WARM_UP = 18
+WARM_UP = 8
 
 
 def tile_conceptembedmodel_pa_kernel(tc, x_words, x_scales, conv_w_words, conv_w_scales, conv_b, out):
@@ -66,23 +65,15 @@ def tile_conceptembedmodel_pa_kernel(tc, x_words, x_scales, conv_w_words, conv_w
         def load_x_planes(r, g0, g1):
             load_planes(x_plane, r, x_scales, g0, g1, N_TILE * r, N_TILE * (r + 1), "xp%d_%d" % (r, g0))
 
-        zeros = keep.tile([P, WARM_N], BF16, name="zeros")
-        nc.gpsimd.memset(zeros[:], 0.0)
-        idle = psum.tile([P, N_TILE], F32, tag="acc", name="idle")
-        for k in range(WARM_UP):
-            nc.tensor.matmul(out=idle[:, 0:WARM_N], lhsT=zeros[:, 0:P], rhs=zeros[:], start=True, stop=True)
-        warm = keep.tile([P, 1], F32, name="warm")
-        nc.scalar.activation(out=warm[:], in_=zeros[:, 0:1], func=EXP)
-
         load_w_planes(0, 1)
+        zeros = keep.tile([P, N_TILE], BF16, name="zeros")
+        nc.vector.memset(zeros[:], 0.0)
         load_w_codes(0, 1)
         load_x_codes(0, 0, 1)
-        load_x_planes(0, 0, 2)
+        load_x_planes(0, 0, PASSES)
         load_w_planes(1, 4)
-        load_x_codes(0, 1, 2)
         load_w_codes(1, 2)
-        load_x_planes(0, 2, 8)
-        load_x_codes(0, 2, 4)
+        load_x_codes(0, 1, 4)
         load_w_codes(2, 4)
         load_w_planes(4, 8)
         load_w_codes(4, 8)
@@ -94,6 +85,12 @@ def tile_conceptembedmodel_pa_kernel(tc, x_words, x_scales, conv_w_words, conv_w
         with nc.allow_non_contiguous_dma(reason="1024 bias values, one channel to a partition"):
             nc.sync.dma_start(out=bias_bf[:], in_=conv_b.rearrange("(c p) -> p c", p=P))
         bias = keep.tile([P, CH_BLOCKS], F32, name="bias")
+
+        idle = psum.tile([P, N_TILE], F32, tag="acc", name="idle")
+        for k in range(WARM_UP):
+            nc.tensor.matmul(out=idle[:], lhsT=zeros[:, 0:P], rhs=zeros[:], start=True, stop=True)
+        warm = keep.tile([P, 1], F32, name="warm")
+        nc.scalar.activation(out=warm[:], in_=zeros[:, 0:1], func=EXP)
 
         peak, neg, pos, ex, val, turned = [], [], [], [], [], []
         for j in range(CH_BLOCKS):

@@ -45,7 +45,7 @@ def tile_conceptembedmodel_pa_kernel(tc, x_words, x_scales, conv_w_words, conv_w
         def load_planes(table, key, scales, g0, g1, c0, c1, name):
             t = keep.tile([P, g1 - g0, c1 - c0], U8, name=name, align_bytes=64)
             nc.vector.memset(t[:].bitcast(I32), 0)
-            for q in range(4):
+            for q in (0, 2, 1, 3):
                 nc.sync.dma_start(
                     out=t[32 * q : 32 * q + 4, :, :].bitcast(I32),
                     in_=scales[g0:g1, 4 * q : 4 * q + 4, c0:c1].rearrange("g r n -> r g n").bitcast(I32),
@@ -65,17 +65,18 @@ def tile_conceptembedmodel_pa_kernel(tc, x_words, x_scales, conv_w_words, conv_w
         def load_x_planes(r, g0, g1):
             load_planes(x_plane, r, x_scales, g0, g1, N_TILE * r, N_TILE * (r + 1), "xp%d_%d" % (r, g0))
 
-        load_w_planes(0, 1)
         zeros = keep.tile([P, N_TILE], BF16, name="zeros")
         nc.vector.memset(zeros[:], 0.0)
-        load_w_codes(0, 1)
         load_x_codes(0, 0, 1)
-        load_x_planes(0, 0, PASSES)
-        load_w_planes(1, 4)
+        load_w_codes(0, 1)
+        load_x_planes(0, 0, 4)
+        load_w_planes(0, 2)
         load_w_codes(1, 2)
         load_x_codes(0, 1, 4)
+        load_w_planes(2, 5)
         load_w_codes(2, 4)
-        load_w_planes(4, 8)
+        load_x_planes(0, 4, 8)
+        load_w_planes(5, 8)
         load_w_codes(4, 8)
         load_x_codes(0, 4, 8)
         for r in range(1, ROW_BLOCKS):
@@ -92,10 +93,9 @@ def tile_conceptembedmodel_pa_kernel(tc, x_words, x_scales, conv_w_words, conv_w
         warm = keep.tile([P, 1], F32, name="warm")
         nc.scalar.activation(out=warm[:], in_=zeros[:, 0:1], func=EXP)
 
-        peak, neg, pos, ex, val, turned = [], [], [], [], [], []
+        peak, pos, ex, val, turned = [], [], [], [], []
         for j in range(CH_BLOCKS):
             peak.append(keep.tile([P, P], F32, name="peak%d" % j))
-            neg.append(keep.tile([P, P], F32, name="neg%d" % j))
             pos.append(keep.tile([P, P], F32, name="pos%d" % j))
             ex.append(keep.tile([P, P], F32, name="ex%d" % j))
             val.append(keep.tile([P, P], F32, name="val%d" % j, align_bytes=64))
@@ -132,27 +132,27 @@ def tile_conceptembedmodel_pa_kernel(tc, x_words, x_scales, conv_w_words, conv_w
             pool_positions(acc, j, r, c0, n)
 
         def elu(j, b0, b1):
-            nc.vector.tensor_scalar(
-                out=neg[j][:, b0:b1], in0=peak[j][:, b0:b1], scalar1=bias[:, j : j + 1], scalar2=0.0,
-                op0=ALU.add, op1=ALU.min,
-            )
-            nc.scalar.activation(out=ex[j][:, b0:b1], in_=neg[j][:, b0:b1], func=EXP)
+            nc.scalar.activation(out=ex[j][:, b0:b1], in_=peak[j][:, b0:b1], func=EXP, bias=bias[:, j : j + 1])
             nc.vector.tensor_scalar(
                 out=pos[j][:, b0:b1], in0=peak[j][:, b0:b1], scalar1=bias[:, j : j + 1], scalar2=0.0,
                 op0=ALU.add, op1=ALU.max,
             )
             nc.vector.scalar_tensor_tensor(
                 out=val[j][:, b0:b1], in0=ex[j][:, b0:b1], scalar=-1.0, in1=pos[j][:, b0:b1],
-                op0=ALU.add, op1=ALU.add,
+                op0=ALU.add, op1=ALU.min,
             )
 
-        def turn_and_store(j, queues):
-            nc.vector.transpose(out=turned[j][:], in_=val[j][:])
+        def turn_and_store(j, queues, t0=0, t1=P // SQ):
+            if t1 - t0 == P // SQ:
+                nc.vector.transpose(out=turned[j][:], in_=val[j][:])
+            else:
+                for t in range(t0, t1):
+                    nc.vector.transpose(out=turned[j][:, SQ * t : SQ * (t + 1)], in_=val[j][:, SQ * t : SQ * (t + 1)])
             for s in range(P // SQ):
                 c0 = P * j + SQ * s
                 queues[s % len(queues)].dma_start(
-                    out=out[:, c0 : c0 + SQ].rearrange("(t i) k -> i t k", i=SQ),
-                    in_=turned[j][SQ * s : SQ * (s + 1), :].rearrange("i (t k) -> i t k", k=SQ),
+                    out=out[SQ * t0 : SQ * t1, c0 : c0 + SQ].rearrange("(t i) k -> i t k", i=SQ),
+                    in_=turned[j][SQ * s : SQ * (s + 1), SQ * t0 : SQ * t1].rearrange("i (t k) -> i t k", k=SQ),
                 )
 
         first = []
@@ -181,11 +181,14 @@ def tile_conceptembedmodel_pa_kernel(tc, x_words, x_scales, conv_w_words, conv_w
             elu(j, 0, P)
             turn_and_store(j, [nc.sync])
 
-        early = (N_TILE // SEQ) * (ROW_BLOCKS - 1)
-        for r in range(1, ROW_BLOCKS - 1):
+        per_block = N_TILE // SEQ
+        for r in range(1, ROW_BLOCKS - 2):
             whole_tile(last, r)
-        elu(last, 0, early)
+        elu(last, 0, per_block * (ROW_BLOCKS - 2))
+        turn_and_store(last, [nc.sync], 0, P // SQ - 1)
+        whole_tile(last, ROW_BLOCKS - 2)
+        elu(last, per_block * (ROW_BLOCKS - 2), per_block * (ROW_BLOCKS - 1))
         whole_tile(last, ROW_BLOCKS - 1, 0, N_TILE // 2)
         whole_tile(last, ROW_BLOCKS - 1, N_TILE // 2, N_TILE // 2)
-        elu(last, early, P)
-        turn_and_store(last, [nc.sync, nc.scalar])
+        elu(last, per_block * (ROW_BLOCKS - 1), P)
+        turn_and_store(last, [nc.sync, nc.scalar], P // SQ - 1, P // SQ)

@@ -20,7 +20,7 @@ ROW_BLOCKS = 8
 CH_BLOCKS = 8
 SIDE_BY_SIDE = 4
 SQ = 32
-WARM_UP = 8
+WARM_UP = 16
 
 
 def tile_conceptembedmodel_pa_kernel(tc, x_words, x_scales, conv_w_words, conv_w_scales, conv_b, out):
@@ -31,7 +31,7 @@ def tile_conceptembedmodel_pa_kernel(tc, x_words, x_scales, conv_w_words, conv_w
         psum = ctx.enter_context(tc.psum_pool(name="psum", bufs=8))
         ctx.enter_context(tc.manual_schedule())
 
-        w_code, w_plane, x_code, x_plane = {}, {}, {}, {}
+        w_code, w_first, w_plane, x_code, x_plane = {}, {}, {}, {}, {}
 
         def load_codes(table, key, words, g0, g1, c0, c1, name):
             t = keep.tile([P, g1 - g0, 2 * (c1 - c0)], U8, name=name, align_bytes=64)
@@ -53,8 +53,12 @@ def tile_conceptembedmodel_pa_kernel(tc, x_words, x_scales, conv_w_words, conv_w
             for g in range(g0, g1):
                 table[(key, g)] = (t, g - g0)
 
-        def load_w_codes(g0, g1):
-            load_codes(w_code, 0, conv_w_words, g0, g1, 0, CH_BLOCKS * P, "wc%d" % g0)
+        def load_w_codes(g0, g1, j0=0, j1=CH_BLOCKS):
+            load_codes(w_code, j0, conv_w_words, g0, g1, P * j0, P * j1, "wc%d_%d" % (g0, j0))
+            for g in range(g0, g1):
+                for j in range(j0, j1):
+                    w_code[(j, g)] = w_code[(j0, g)]
+                    w_first[(j, g)] = j0
 
         def load_w_planes(g0, g1):
             load_planes(w_plane, 0, conv_w_scales, g0, g1, 0, CH_BLOCKS * P, "wp%d" % g0)
@@ -68,9 +72,10 @@ def tile_conceptembedmodel_pa_kernel(tc, x_words, x_scales, conv_w_words, conv_w
         zeros = keep.tile([P, N_TILE], BF16, name="zeros")
         nc.vector.memset(zeros[:], 0.0)
         load_x_codes(0, 0, 1)
-        load_w_codes(0, 1)
+        load_w_codes(0, 1, 0, CH_BLOCKS // 2)
         load_x_planes(0, 0, 4)
         load_w_planes(0, 2)
+        load_w_codes(0, 1, CH_BLOCKS // 2, CH_BLOCKS)
         load_w_codes(1, 2)
         load_x_codes(0, 1, 4)
         load_w_planes(2, 5)
@@ -102,13 +107,14 @@ def tile_conceptembedmodel_pa_kernel(tc, x_words, x_scales, conv_w_words, conv_w
             turned.append(keep.tile([P, P], F32, name="turned%d" % j, align_bytes=64))
 
         def multiply(acc, j, r, g, c0, n):
-            wc, wi = w_code[(0, g)]
+            wc, wi = w_code[(j, g)]
+            wj = j - w_first[(j, g)]
             wp, wpi = w_plane[(0, g)]
             xc, xi = x_code[(r, g)]
             xp, xpi = x_plane[(r, g)]
             nc.tensor.matmul_mx(
                 out=acc[:, 0:n],
-                lhsT=wc[:, wi, 2 * P * j : 2 * P * (j + 1)].bitcast(FP4X4),
+                lhsT=wc[:, wi, 2 * P * wj : 2 * P * (wj + 1)].bitcast(FP4X4),
                 lhsT_scale=wp[:, wpi, P * j : P * (j + 1)],
                 rhs=xc[:, xi, 2 * c0 : 2 * (c0 + n)].bitcast(FP4X4),
                 rhs_scale=xp[:, xpi, c0 : c0 + n],

@@ -78,12 +78,13 @@ def tile_conceptembedmodel_pa_kernel(tc, x_words, x_scales, conv_w_words, conv_w
         load_w_codes(0, 1, CH_BLOCKS // 2, CH_BLOCKS)
         load_w_codes(1, 2)
         load_x_codes(0, 1, 4)
-        load_w_planes(2, 5)
         load_w_codes(2, 4)
+        load_w_planes(2, 5)
+        load_x_codes(0, 4, 8)
+        load_w_codes(4, 6)
         load_x_planes(0, 4, 8)
         load_w_planes(5, 8)
-        load_w_codes(4, 8)
-        load_x_codes(0, 4, 8)
+        load_w_codes(6, 8)
         for r in range(1, ROW_BLOCKS):
             load_x_planes(r, 0, PASSES)
             load_x_codes(r, 0, PASSES)

@@ -20,7 +20,6 @@ ROW_BLOCKS = 8
 CH_BLOCKS = 8
 SIDE_BY_SIDE = 4
 SQ = 32
-WARM_UP = 16
 
 
 def tile_conceptembedmodel_pa_kernel(tc, x_words, x_scales, conv_w_words, conv_w_scales, conv_b, out):
@@ -93,9 +92,6 @@ def tile_conceptembedmodel_pa_kernel(tc, x_words, x_scales, conv_w_words, conv_w
             nc.sync.dma_start(out=bias_bf[:], in_=conv_b.rearrange("(c p) -> p c", p=P))
         bias = keep.tile([P, CH_BLOCKS], F32, name="bias")
 
-        idle = psum.tile([P, N_TILE], F32, tag="acc", name="idle")
-        for k in range(WARM_UP):
-            nc.tensor.matmul(out=idle[:], lhsT=zeros[:, 0:P], rhs=zeros[:], start=True, stop=True)
         warm = keep.tile([P, 1], F32, name="warm")
         nc.scalar.activation(out=warm[:], in_=zeros[:, 0:1], func=EXP)
 

@@ -16,10 +16,13 @@ P = 128
 PASSES = 8
 SEQ = 32
 N_TILE = 512
+SEQS_OF_A_ROW_BLOCK = N_TILE // SEQ
 ROW_BLOCKS = 8
 CH_BLOCKS = 8
+BANKS = 8
 SIDE_BY_SIDE = 4
 SQ = 32
+SQUARES = P // SQ
 
 
 def tile_conceptembedmodel_pa_kernel(tc, x_words, x_scales, conv_w_words, conv_w_scales, conv_b, out):
@@ -27,49 +30,50 @@ def tile_conceptembedmodel_pa_kernel(tc, x_words, x_scales, conv_w_words, conv_w
 
     with ExitStack() as ctx:
         keep = ctx.enter_context(tc.tile_pool(name="keep", bufs=1))
-        psum = ctx.enter_context(tc.psum_pool(name="psum", bufs=8))
+        psum = ctx.enter_context(tc.psum_pool(name="psum", bufs=BANKS))
         ctx.enter_context(tc.manual_schedule())
 
-        w_code, w_first, w_plane, x_code, x_plane = {}, {}, {}, {}, {}
+        w_code = {}
+        w_plane = {}
+        x_code = {}
+        x_plane = {}
 
-        def load_codes(table, key, words, g0, g1, c0, c1, name):
-            t = keep.tile([P, g1 - g0, 2 * (c1 - c0)], U8, name=name, align_bytes=64)
+        def load_codes(table, words, g0, g1, first, blocks, width, name):
+            t = keep.tile([P, g1 - g0, 2 * width * blocks], U8, name=name, align_bytes=64)
             nc.sync.dma_start(
                 out=t[:].bitcast(I32),
-                in_=words[g0:g1, :, 2 * c0 : 2 * c1].rearrange("g p n -> p g n").bitcast(I32),
+                in_=words[g0:g1, :, 2 * width * first : 2 * width * (first + blocks)].rearrange("g p n -> p g n").bitcast(I32),
             )
             for g in range(g0, g1):
-                table[(key, g)] = (t, g - g0)
+                for k in range(blocks):
+                    table[(first + k, g)] = t[:, g - g0, 2 * width * k : 2 * width * (k + 1)]
 
-        def load_planes(table, key, scales, g0, g1, c0, c1, name):
-            t = keep.tile([P, g1 - g0, c1 - c0], U8, name=name, align_bytes=64)
+        def load_planes(table, scales, g0, g1, first, blocks, width, name):
+            t = keep.tile([P, g1 - g0, width * blocks], U8, name=name, align_bytes=64)
             nc.vector.memset(t[:].bitcast(I32), 0)
             for q in (0, 2, 1, 3):
                 nc.sync.dma_start(
                     out=t[32 * q : 32 * q + 4, :, :].bitcast(I32),
-                    in_=scales[g0:g1, 4 * q : 4 * q + 4, c0:c1].rearrange("g r n -> r g n").bitcast(I32),
+                    in_=scales[g0:g1, 4 * q : 4 * q + 4, width * first : width * (first + blocks)]
+                    .rearrange("g i n -> i g n")
+                    .bitcast(I32),
                 )
             for g in range(g0, g1):
-                table[(key, g)] = (t, g - g0)
+                for k in range(blocks):
+                    table[(first + k, g)] = t[:, g - g0, width * k : width * (k + 1)]
 
         def load_w_codes(g0, g1, j0=0, j1=CH_BLOCKS):
-            load_codes(w_code, j0, conv_w_words, g0, g1, P * j0, P * j1, "wc%d_%d" % (g0, j0))
-            for g in range(g0, g1):
-                for j in range(j0, j1):
-                    w_code[(j, g)] = w_code[(j0, g)]
-                    w_first[(j, g)] = j0
+            load_codes(w_code, conv_w_words, g0, g1, j0, j1 - j0, P, "wc%d_%d" % (g0, j0))
 
         def load_w_planes(g0, g1):
-            load_planes(w_plane, 0, conv_w_scales, g0, g1, 0, CH_BLOCKS * P, "wp%d" % g0)
+            load_planes(w_plane, conv_w_scales, g0, g1, 0, CH_BLOCKS, P, "wp%d" % g0)
 
         def load_x_codes(r, g0, g1):
-            load_codes(x_code, r, x_words, g0, g1, N_TILE * r, N_TILE * (r + 1), "xc%d_%d" % (r, g0))
+            load_codes(x_code, x_words, g0, g1, r, 1, N_TILE, "xc%d_%d" % (r, g0))
 
         def load_x_planes(r, g0, g1):
-            load_planes(x_plane, r, x_scales, g0, g1, N_TILE * r, N_TILE * (r + 1), "xp%d_%d" % (r, g0))
+            load_planes(x_plane, x_scales, g0, g1, r, 1, N_TILE, "xp%d_%d" % (r, g0))
 
-        zeros = keep.tile([P, N_TILE], BF16, name="zeros")
-        nc.vector.memset(zeros[:], 0.0)
         load_x_codes(0, 0, 1)
         load_w_codes(0, 1, 0, CH_BLOCKS // 2)
         load_x_planes(0, 0, 4)
@@ -92,9 +96,6 @@ def tile_conceptembedmodel_pa_kernel(tc, x_words, x_scales, conv_w_words, conv_w
             nc.sync.dma_start(out=bias_bf[:], in_=conv_b.rearrange("(c p) -> p c", p=P))
         bias = keep.tile([P, CH_BLOCKS], F32, name="bias")
 
-        warm = keep.tile([P, 1], F32, name="warm")
-        nc.scalar.activation(out=warm[:], in_=zeros[:, 0:1], func=EXP)
-
         peak, pos, ex, val, turned = [], [], [], [], []
         for j in range(CH_BLOCKS):
             peak.append(keep.tile([P, P], F32, name="peak%d" % j))
@@ -104,17 +105,12 @@ def tile_conceptembedmodel_pa_kernel(tc, x_words, x_scales, conv_w_words, conv_w
             turned.append(keep.tile([P, P], F32, name="turned%d" % j, align_bytes=64))
 
         def multiply(acc, j, r, g, c0, n):
-            wc, wi = w_code[(j, g)]
-            wj = j - w_first[(j, g)]
-            wp, wpi = w_plane[(0, g)]
-            xc, xi = x_code[(r, g)]
-            xp, xpi = x_plane[(r, g)]
             nc.tensor.matmul_mx(
                 out=acc[:, 0:n],
-                lhsT=wc[:, wi, 2 * P * wj : 2 * P * (wj + 1)].bitcast(FP4X4),
-                lhsT_scale=wp[:, wpi, P * j : P * (j + 1)],
-                rhs=xc[:, xi, 2 * c0 : 2 * (c0 + n)].bitcast(FP4X4),
-                rhs_scale=xp[:, xpi, c0 : c0 + n],
+                lhsT=w_code[(j, g)].bitcast(FP4X4),
+                lhsT_scale=w_plane[(j, g)],
+                rhs=x_code[(r, g)][:, 2 * c0 : 2 * (c0 + n)].bitcast(FP4X4),
+                rhs_scale=x_plane[(r, g)][:, c0 : c0 + n],
                 start=(g == 0),
                 stop=(g == PASSES - 1),
             )
@@ -145,13 +141,13 @@ def tile_conceptembedmodel_pa_kernel(tc, x_words, x_scales, conv_w_words, conv_w
                 op0=ALU.add, op1=ALU.min,
             )
 
-        def turn_and_store(j, queues, t0=0, t1=P // SQ):
-            if t1 - t0 == P // SQ:
+        def turn_and_store(j, queues, t0=0, t1=SQUARES):
+            if t1 - t0 == SQUARES:
                 nc.vector.transpose(out=turned[j][:], in_=val[j][:])
             else:
                 for t in range(t0, t1):
                     nc.vector.transpose(out=turned[j][:, SQ * t : SQ * (t + 1)], in_=val[j][:, SQ * t : SQ * (t + 1)])
-            for s in range(P // SQ):
+            for s in range(SQUARES):
                 c0 = P * j + SQ * s
                 queues[s % len(queues)].dma_start(
                     out=out[SQ * t0 : SQ * t1, c0 : c0 + SQ].rearrange("(t i) k -> i t k", i=SQ),
@@ -184,14 +180,13 @@ def tile_conceptembedmodel_pa_kernel(tc, x_words, x_scales, conv_w_words, conv_w
             elu(j, 0, P)
             turn_and_store(j, [nc.sync])
 
-        per_block = N_TILE // SEQ
         for r in range(1, ROW_BLOCKS - 2):
             whole_tile(last, r)
-        elu(last, 0, per_block * (ROW_BLOCKS - 2))
-        turn_and_store(last, [nc.sync], 0, P // SQ - 1)
+        elu(last, 0, SEQS_OF_A_ROW_BLOCK * (ROW_BLOCKS - 2))
+        turn_and_store(last, [nc.sync], 0, SQUARES - 1)
         whole_tile(last, ROW_BLOCKS - 2)
-        elu(last, per_block * (ROW_BLOCKS - 2), per_block * (ROW_BLOCKS - 1))
+        elu(last, SEQS_OF_A_ROW_BLOCK * (ROW_BLOCKS - 2), SEQS_OF_A_ROW_BLOCK * (ROW_BLOCKS - 1))
         whole_tile(last, ROW_BLOCKS - 1, 0, N_TILE // 2)
         whole_tile(last, ROW_BLOCKS - 1, N_TILE // 2, N_TILE // 2)
-        elu(last, per_block * (ROW_BLOCKS - 1), P)
-        turn_and_store(last, [nc.sync, nc.scalar], P // SQ - 1, P // SQ)
+        elu(last, SEQS_OF_A_ROW_BLOCK * (ROW_BLOCKS - 1), P)
+        turn_and_store(last, [nc.sync, nc.scalar], SQUARES - 1, SQUARES)

@@ -147,6 +147,12 @@ def tile_conceptembedmodel_pa_kernel(tc, x_words, x_scales, conv_w_words, conv_w
             else:
                 for t in range(t0, t1):
                     nc.vector.transpose(out=turned[j][:, SQ * t : SQ * (t + 1)], in_=val[j][:, SQ * t : SQ * (t + 1)])
+            if t1 - t0 == 1:
+                queues[0].dma_start(
+                    out=out[SQ * t0 : SQ * t1, P * j : P * (j + 1)].rearrange("i (s k) -> s i k", k=SQ),
+                    in_=turned[j][:, SQ * t0 : SQ * t1],
+                )
+                return
             for s in range(SQUARES):
                 c0 = P * j + SQ * s
                 queues[s % len(queues)].dma_start(

@@ -76,17 +76,18 @@ def tile_conceptembedmodel_pa_kernel(tc, x_words, x_scales, conv_w_words, conv_w
 
         load_x_codes(0, 0, 1)
         load_w_codes(0, 1, 0, CH_BLOCKS // 2)
-        load_x_planes(0, 0, 4)
-        load_w_planes(0, 2)
+        load_x_planes(0, 0, 2)
+        load_w_planes(0, 1)
         load_w_codes(0, 1, CH_BLOCKS // 2, CH_BLOCKS)
-        load_w_codes(1, 2)
         load_x_codes(0, 1, 4)
+        load_w_codes(1, 2)
+        load_w_planes(1, 3)
         load_w_codes(2, 4)
-        load_w_planes(2, 5)
+        load_x_planes(0, 2, 8)
+        load_w_planes(3, 6)
         load_x_codes(0, 4, 8)
         load_w_codes(4, 6)
-        load_x_planes(0, 4, 8)
-        load_w_planes(5, 8)
+        load_w_planes(6, 8)
         load_w_codes(6, 8)
         for r in range(1, ROW_BLOCKS):
             load_x_planes(r, 0, PASSES)

@@ -194,6 +194,7 @@ def tile_conceptembedmodel_pa_kernel(tc, x_words, x_scales, conv_w_words, conv_w
         whole_tile(last, ROW_BLOCKS - 2)
         elu(last, SEQS_OF_A_ROW_BLOCK * (ROW_BLOCKS - 2), SEQS_OF_A_ROW_BLOCK * (ROW_BLOCKS - 1))
         whole_tile(last, ROW_BLOCKS - 1, 0, N_TILE // 2)
-        whole_tile(last, ROW_BLOCKS - 1, N_TILE // 2, N_TILE // 2)
+        whole_tile(last, ROW_BLOCKS - 1, N_TILE // 2, N_TILE // 4)
+        whole_tile(last, ROW_BLOCKS - 1, 3 * N_TILE // 4, N_TILE // 4)
         elu(last, SEQS_OF_A_ROW_BLOCK * (ROW_BLOCKS - 1), P)
         turn_and_store(last, [nc.sync, nc.scalar], SQUARES - 1, SQUARES)

from contextlib import ExitStack

import concourse.mybir as mybir

FLOPS = 2 * 4096 * 1024 * 4096

F32 = mybir.dt.float32
BF16 = mybir.dt.bfloat16
I32 = mybir.dt.int32
U8 = mybir.dt.uint8
FP4X4 = mybir.dt.float4_e2m1fn_x4
ALU = mybir.AluOpType
EXP = mybir.ActivationFunctionType.Exp

P = 128
PASSES = 8
SEQ = 32
N_TILE = 512
SEQS_OF_A_ROW_BLOCK = N_TILE // SEQ
ROW_BLOCKS = 8
CH_BLOCKS = 8
BANKS = 8
SIDE_BY_SIDE = 4
SQ = 32
SQUARES = P // SQ


def tile_conceptembedmodel_pa_kernel(tc, x_words, x_scales, conv_w_words, conv_w_scales, conv_b, out):
    nc = tc.nc

    with ExitStack() as ctx:
        keep = ctx.enter_context(tc.tile_pool(name="keep", bufs=1))
        psum = ctx.enter_context(tc.psum_pool(name="psum", bufs=BANKS))
        ctx.enter_context(tc.manual_schedule())

        w_code = {}
        w_plane = {}
        x_code = {}
        x_plane = {}

        def load_codes(table, words, g0, g1, first, blocks, width, name):
            t = keep.tile([P, g1 - g0, 2 * width * blocks], U8, name=name, align_bytes=64)
            nc.sync.dma_start(
                out=t[:].bitcast(I32),
                in_=words[g0:g1, :, 2 * width * first : 2 * width * (first + blocks)].rearrange("g p n -> p g n").bitcast(I32),
            )
            for g in range(g0, g1):
                for k in range(blocks):
                    table[(first + k, g)] = t[:, g - g0, 2 * width * k : 2 * width * (k + 1)]

        def load_planes(table, scales, g0, g1, first, blocks, width, name):
            t = keep.tile([P, g1 - g0, width * blocks], U8, name=name, align_bytes=64)
            nc.vector.memset(t[:].bitcast(I32), 0)
            for q in (0, 2, 1, 3):
                nc.sync.dma_start(
                    out=t[32 * q : 32 * q + 4, :, :].bitcast(I32),
                    in_=scales[g0:g1, 4 * q : 4 * q + 4, width * first : width * (first + blocks)]
                    .rearrange("g i n -> i g n")
                    .bitcast(I32),
                )
            for g in range(g0, g1):
                for k in range(blocks):
                    table[(first + k, g)] = t[:, g - g0, width * k : width * (k + 1)]

        def load_w_codes(g0, g1, j0=0, j1=CH_BLOCKS):
            load_codes(w_code, conv_w_words, g0, g1, j0, j1 - j0, P, "wc%d_%d" % (g0, j0))

        def load_w_planes(g0, g1):
            load_planes(w_plane, conv_w_scales, g0, g1, 0, CH_BLOCKS, P, "wp%d" % g0)

        def load_x_codes(r, g0, g1):
            load_codes(x_code, x_words, g0, g1, r, 1, N_TILE, "xc%d_%d" % (r, g0))

        def load_x_planes(r, g0, g1):
            load_planes(x_plane, x_scales, g0, g1, r, 1, N_TILE, "xp%d_%d" % (r, g0))

        load_x_codes(0, 0, 1)
        load_w_codes(0, 1, 0, CH_BLOCKS // 2)
        load_x_planes(0, 0, 2)
        load_w_planes(0, 1)
        load_w_codes(0, 1, CH_BLOCKS // 2, CH_BLOCKS)
        load_x_codes(0, 1, 4)
        load_w_codes(1, 2)
        load_w_planes(1, 3)
        load_w_codes(2, 4)
        load_x_planes(0, 2, 8)
        load_w_planes(3, 6)
        load_x_codes(0, 4, 8)
        load_w_codes(4, 6)
        load_w_planes(6, 8)
        load_w_codes(6, 8)
        for r in range(1, ROW_BLOCKS):
            load_x_planes(r, 0, PASSES)
            load_x_codes(r, 0, PASSES)
        bias_bf = keep.tile([P, CH_BLOCKS], BF16, name="bias_bf")
        with nc.allow_non_contiguous_dma(reason="1024 bias values, one channel to a partition"):
            nc.sync.dma_start(out=bias_bf[:], in_=conv_b.rearrange("(c p) -> p c", p=P))
        bias = keep.tile([P, CH_BLOCKS], F32, name="bias")

        peak, pos, ex, val, turned = [], [], [], [], []
        for j in range(CH_BLOCKS):
            peak.append(keep.tile([P, P], F32, name="peak%d" % j))
            pos.append(keep.tile([P, P], F32, name="pos%d" % j))
            ex.append(keep.tile([P, P], F32, name="ex%d" % j))
            val.append(keep.tile([P, P], F32, name="val%d" % j, align_bytes=64))
            turned.append(keep.tile([P, P], F32, name="turned%d" % j, align_bytes=64))

        def multiply(acc, j, r, g, c0, n):
            nc.tensor.matmul_mx(
                out=acc[:, 0:n],
                lhsT=w_code[(j, g)].bitcast(FP4X4),
                lhsT_scale=w_plane[(j, g)],
                rhs=x_code[(r, g)][:, 2 * c0 : 2 * (c0 + n)].bitcast(FP4X4),
                rhs_scale=x_plane[(r, g)][:, c0 : c0 + n],
                start=(g == 0),
                stop=(g == PASSES - 1),
            )

        def pool_positions(acc, j, r, c0, n):
            b0 = (N_TILE * r + c0) // SEQ
            nc.vector.tensor_reduce(
                out=peak[j][:, b0 : b0 + n // SEQ],
                in_=acc[:, 0:n].rearrange("p (b l) -> p b l", l=SEQ),
                axis=mybir.AxisListType.X,
                op=ALU.max,
            )

        def whole_tile(j, r, c0=0, n=N_TILE):
            acc = psum.tile([P, N_TILE], F32, tag="acc", name="acc")
            for g in range(PASSES):
                multiply(acc, j, r, g, c0, n)
            pool_positions(acc, j, r, c0, n)

        def elu(j, b0, b1):
            nc.scalar.activation(out=ex[j][:, b0:b1], in_=peak[j][:, b0:b1], func=EXP, bias=bias[:, j : j + 1])
            nc.vector.tensor_scalar(
                out=pos[j][:, b0:b1], in0=peak[j][:, b0:b1], scalar1=bias[:, j : j + 1], scalar2=0.0,
                op0=ALU.add, op1=ALU.max,
            )
            nc.vector.scalar_tensor_tensor(
                out=val[j][:, b0:b1], in0=ex[j][:, b0:b1], scalar=-1.0, in1=pos[j][:, b0:b1],
                op0=ALU.add, op1=ALU.min,
            )

        def turn_and_store(j, queues, t0=0, t1=SQUARES):
            if t1 - t0 == SQUARES:
                nc.vector.transpose(out=turned[j][:], in_=val[j][:])
            else:
                for t in range(t0, t1):
                    nc.vector.transpose(out=turned[j][:, SQ * t : SQ * (t + 1)], in_=val[j][:, SQ * t : SQ * (t + 1)])
            if t1 - t0 == 1:
                queues[0].dma_start(
                    out=out[SQ * t0 : SQ * t1, P * j : P * (j + 1)].rearrange("i (s k) -> s i k", k=SQ),
                    in_=turned[j][:, SQ * t0 : SQ * t1],
                )
                return
            for s in range(SQUARES):
                c0 = P * j + SQ * s
                queues[s % len(queues)].dma_start(
                    out=out[SQ * t0 : SQ * t1, c0 : c0 + SQ].rearrange("(t i) k -> i t k", i=SQ),
                    in_=turned[j][SQ * s : SQ * (s + 1), SQ * t0 : SQ * t1].rearrange("i (t k) -> i t k", k=SQ),
                )

        first = []
        for j in range(CH_BLOCKS):
            acc0 = psum.tile([P, N_TILE], F32, tag="acc", name="acc")
            first.append(acc0)
        for g in range(PASSES):
            for j in range(CH_BLOCKS):
                multiply(first[j], j, 0, g, 0, N_TILE)
        for j in range(CH_BLOCKS):
            pool_positions(first[j], j, 0, 0, N_TILE)

        for r in range(1, ROW_BLOCKS):
            if r == ROW_BLOCKS - 1:
                nc.vector.tensor_copy(out=bias[:], in_=bias_bf[:])
            for j in range(SIDE_BY_SIDE):
                whole_tile(j, r)
                if r == ROW_BLOCKS - 1:
                    elu(j, 0, P)
                    turn_and_store(j, [nc.sync])

        last = CH_BLOCKS - 1
        for j in range(SIDE_BY_SIDE, last):
            for r in range(1, ROW_BLOCKS):
                whole_tile(j, r)
            elu(j, 0, P)
            turn_and_store(j, [nc.sync])

        for r in range(1, ROW_BLOCKS - 2):
            whole_tile(last, r)
        elu(last, 0, SEQS_OF_A_ROW_BLOCK * (ROW_BLOCKS - 2))
        turn_and_store(last, [nc.sync], 0, SQUARES - 1)
        whole_tile(last, ROW_BLOCKS - 2)
        elu(last, SEQS_OF_A_ROW_BLOCK * (ROW_BLOCKS - 2), SEQS_OF_A_ROW_BLOCK * (ROW_BLOCKS - 1))
        whole_tile(last, ROW_BLOCKS - 1, 0, N_TILE // 2)
        whole_tile(last, ROW_BLOCKS - 1, N_TILE // 2, N_TILE // 4)
        whole_tile(last, ROW_BLOCKS - 1, 3 * N_TILE // 4, N_TILE // 4)
        elu(last, SEQS_OF_A_ROW_BLOCK * (ROW_BLOCKS - 1), P)
        turn_and_store(last, [nc.sync, nc.scalar], SQUARES - 1, SQUARES)
